import numpy as np
import ml_dtypes


def mxq(x, axis, fmt="e4m3"):
    dtype, down = {"e4m3": (ml_dtypes.float8_e4m3fn, 7), "e5m2": (ml_dtypes.float8_e5m2, 14)}[fmt]
    v = np.moveaxis(np.asarray(x, np.float32).astype(ml_dtypes.bfloat16).astype(np.float64), axis, -1)
    blocks = v.reshape(v.shape[:-1] + (-1, 32))
    amax = np.abs(blocks).max(-1, keepdims=True)
    byte = np.maximum(np.where(amax > 0, np.frexp(amax)[1] - 1 + 127, 0) - down, 1)
    scale = np.exp2(byte - 127.0)
    codes = (blocks / scale).astype(np.float32).astype(dtype).astype(np.float64)
    return np.moveaxis((codes * scale).reshape(v.shape), -1, axis)


WIDE = False


def mx_kscale(k):
    if not WIDE:
        return np.ones(k)
    levels = np.array([10, -10, 5, -5, 0])
    a = np.random.permutation(np.resize(levels, k // 512 * 4)).reshape(k // 512, 4)
    idx = np.arange(k)
    return np.exp2(a[idx // 512, idx % 128 // 32])


BF16 = ml_dtypes.bfloat16


def bf(x):
    return np.asarray(x, np.float32).astype(BF16)


def f64(x):
    return np.asarray(x).astype(np.float64)


B, N, C, H = 1, 1536, 2048, 1024
EPS = 1e-12


def layer_norm(v, w, b):
    u = v.mean(-1, keepdims=True)
    s = ((v - u) ** 2).mean(-1, keepdims=True)
    return w * ((v - u) / np.sqrt(s + EPS)) + b


def setup_inputs():
    s = mx_kscale(C)
    x = np.random.standard_normal((B, N, C)) * (0.4 + 1.2 * np.random.random((B, N)))[:, :, None] + 0.4 * np.random.standard_normal((B, N))[:, :, None]
    return {"x": bf(x),
            "pre_w": bf((1.0 + 0.1 * np.random.standard_normal(C)) * s),
            "pre_b": bf(0.2 * np.random.standard_normal(C) * s),
            "lin1_W": bf(np.random.standard_normal((H, C)) / np.sqrt(C) / s[None, :]),
            "lin1_b": bf(0.3 * np.random.standard_normal(H) + 0.3),
            "n1_w": bf(1.0 + 0.1 * np.random.standard_normal(H)),
            "n1_b": bf(0.2 * np.random.standard_normal(H))}


def reference(x, pre_w, pre_b, lin1_W, lin1_b, n1_w, n1_b):
    y = np.maximum(layer_norm(f64(x), f64(pre_w), f64(pre_b)), 0.0)
    y = (mxq(y, 2, "e4m3") @ mxq(f64(lin1_W), 1, "e4m3").T) + f64(lin1_b)
    return np.maximum(layer_norm(y, f64(n1_w), f64(n1_b)), 0.0)

@@ -1,0 +1,233 @@
+from contextlib import ExitStack
+
+import concourse.mybir as mybir
+from concourse.masks import make_identity
+
+F32 = mybir.dt.float32
+BF16 = mybir.dt.bfloat16
+I32 = mybir.dt.int32
+U32 = mybir.dt.uint32
+U8 = mybir.dt.uint8
+FP8X4 = mybir.dt.float8_e4m3fn_x4
+ACT = mybir.ActivationFunctionType
+ALU = mybir.AluOpType
+
+P = 128
+TOKENS = 1536
+C = 2048
+H = 1024
+EPS = 1e-12
+PACK = 4
+K_PASS = P * PACK
+PASSES = C // K_PASS
+BLOCKS = C // P
+GROUP = 4
+GROUP_TOKENS = GROUP * P
+GROUPS = TOKENS // GROUP_TOKENS
+N_COLS = 512
+HALVES = H // N_COLS
+BN_CHUNK = 512
+
+FLOPS = 2 * TOKENS * C * H
+
+
+def tile_graphresblock_pa_kernel(tc, x, pre_w, pre_b, lin1_W, lin1_b, n1_w, n1_b, out):
+    nc = tc.nc
+    x_rows = x.flatten_outer_dims()
+    out_rows = out.flatten_outer_dims()
+
+    with ExitStack() as stack:
+        const = stack.enter_context(tc.tile_pool(name="const", bufs=1))
+        small = stack.enter_context(tc.tile_pool(name="small", bufs=6))
+        x_pool = stack.enter_context(tc.tile_pool(name="x_pool", bufs=6))
+        w_pool = stack.enter_context(tc.tile_pool(name="w_pool", bufs=4))
+        xn_pool = stack.enter_context(tc.tile_pool(name="xn_pool", bufs=8))
+        stage = stack.enter_context(tc.tile_pool(name="stage", bufs=3))
+        y_pool = stack.enter_context(tc.tile_pool(name="y_pool", bufs=2))
+        z_pool = stack.enter_context(tc.tile_pool(name="z_pool", bufs=3))
+        psum_t = stack.enter_context(tc.psum_pool(name="psum_t", bufs=4))
+        psum_acc = stack.enter_context(tc.psum_pool(name="psum_acc", bufs=4))
+
+        ident = const.tile([P, P], F32)
+        make_identity(nc, ident[:])
+        eps_col = const.tile([P, 1], F32)
+        nc.vector.memset(eps_col[:], EPS)
+        table_warm = const.tile([P, 1], F32)
+        nc.scalar.activation(out=table_warm[:], in_=eps_col[:], func=ACT.Sqrt)
+
+        wb_rows = const.tile([P, 2 * P], BF16)
+        nc.vector.memset(wb_rows[:].bitcast(I32), 0)
+        nc.sync.dma_start(out=wb_rows[0:8, :], in_=pre_w.rearrange("(a c) -> a c", c=2 * P))
+        nc.sync.dma_start(out=wb_rows[8:16, :], in_=pre_b.rearrange("(a c) -> a c", c=2 * P))
+
+        bias_b = const.tile([P, H], BF16)
+        gain_b = const.tile([P, H], BF16)
+        shift_b = const.tile([P, H], BF16)
+        nc.gpsimd.dma_start(out=bias_b[:], in_=lin1_b.partition_broadcast(P))
+        nc.gpsimd.dma_start(out=gain_b[:], in_=n1_w.partition_broadcast(P))
+        nc.gpsimd.dma_start(out=shift_b[:], in_=n1_b.partition_broadcast(P))
+
+        x_nat = {}
+        w_nat = {}
+
+        def load_x(i):
+            x_nat[i] = x_pool.tile([P, C], BF16, name="x_nat")
+            nc.sync.dma_start(out=x_nat[i][:], in_=x_rows[P * i : P * i + P, :])
+
+        def load_w(r):
+            w_nat[r] = w_pool.tile([P, C], BF16, name="w_nat")
+            nc.sync.dma_start(out=w_nat[r][:], in_=lin1_W[P * r : P * r + P, :])
+
+        for i in range(GROUP):
+            load_x(i)
+            load_w(2 * i)
+            load_w(2 * i + 1)
+
+        wb_t = psum_t.tile([P, N_COLS], F32, tag="t")
+        nc.tensor.transpose(wb_t[:, 0:P], wb_rows[:].bitcast(F32), ident[:])
+        wb_pairs = const.tile([P, 2 * BLOCKS], BF16)
+        nc.vector.tensor_copy(out=wb_pairs[:].bitcast(F32), in_=wb_t[:, 0:BLOCKS])
+        wb_cols = const.tile([P, 2 * BLOCKS], F32)
+        nc.vector.tensor_copy(out=wb_cols[:], in_=wb_pairs[:])
+
+        xn = {}
+
+        def normalise(i):
+            stats = small.tile([P, C // BN_CHUNK, 6], F32, name="stats")
+            for s in range(C // BN_CHUNK):
+                nc.vector.bn_stats(out=stats[:, s, :], in_=x_nat[i][:, BN_CHUNK * s : BN_CHUNK * (s + 1)])
+            mean_var = small.tile([P, 2], F32, name="mean_var")
+            nc.vector.bn_aggr(out=mean_var[:], in_=stats[:].rearrange("p s d -> p (s d)"))
+            std = small.tile([P, 1], F32, name="std")
+            nc.scalar.activation(out=std[:], in_=mean_var[:, 1:2], func=ACT.Sqrt, bias=eps_col[:], scale=1.0)
+            rstd = small.tile([P, 1], F32, name="rstd")
+            nc.vector.reciprocal(out=rstd[:], in_=std[:])
+            shift = small.tile([P, 1], F32, name="shift")
+            nc.vector.scalar_tensor_tensor(
+                out=shift[:], in0=mean_var[:, 0:1], scalar=-1.0, in1=rstd[:], op0=ALU.mult, op1=ALU.mult
+            )
+            xn[i] = xn_pool.tile([P, BLOCKS, P], F32, name="xn")
+            nc.scalar.activation(
+                out=xn[i][:].rearrange("p (a e) q -> p a e q", e=2),
+                in_=x_nat[i][:].rearrange("p (a q e) -> p a e q", q=P, e=2),
+                func=ACT.Identity,
+                scale=rstd[:],
+                bias=shift[:],
+            )
+
+        w_words = const.tile([P, PASSES, H], U32, align_bytes=64)
+        w_scales = const.tile([P, PASSES, H], U8, align_bytes=64)
+
+        def quantise_w(pair):
+            for g in range(PASSES):
+                wt = psum_t.tile([P, 2, 2 * P], F32, tag="t")
+                for u in range(2):
+                    for r in range(2):
+                        words = w_nat[2 * pair + r][:].bitcast(F32)
+                        first = P * (2 * g + u)
+                        nc.tensor.transpose(wt[:, u, P * r : P * r + P], words[:, first : first + P], ident[:])
+                w_grouped = stage.tile([P, 2 * P * PACK], BF16, align_bytes=64, name="w_grouped")
+                nc.scalar.copy(
+                    out=w_grouped[:].bitcast(F32).rearrange("p (h u) -> p h u", u=2),
+                    in_=wt[:].rearrange("p u h -> p h u"),
+                )
+                cols = slice(2 * P * pair, 2 * P * (pair + 1))
+                nc.vector.quantize_mx(
+                    out=w_words[:, g, cols].bitcast(FP8X4), scales=w_scales[:, g, cols], in_=w_grouped[:]
+                )
+
+        def quantise_y(group):
+            y_words = y_pool.tile([P, PASSES, GROUP_TOKENS], U32, align_bytes=64, name="y_words")
+            y_scales = y_pool.tile([P, PASSES, GROUP_TOKENS], U8, align_bytes=64, name="y_scales")
+            for g in range(PASSES):
+                y_planes = stage.tile([P, PACK, GROUP_TOKENS], BF16, name="y_planes")
+                for t in range(PACK):
+                    j = PACK * g + t
+                    xt = psum_t.tile([P, GROUP_TOKENS], F32, tag="t")
+                    for i in range(GROUP):
+                        nc.tensor.transpose(xt[:, P * i : P * i + P], xn[GROUP * group + i][:, j, :], ident[:])
+                    nc.scalar.activation(
+                        out=y_planes[:, t, :],
+                        in_=xt[:],
+                        func=ACT.Relu,
+                        scale=wb_cols[:, j : j + 1],
+                        bias=wb_cols[:, BLOCKS + j : BLOCKS + j + 1],
+                    )
+                y_grouped = stage.tile([P, GROUP_TOKENS * PACK], BF16, align_bytes=64, name="y_grouped")
+                nc.vector.tensor_copy(
+                    out=y_grouped[:].rearrange("p (c i t) -> p c t i", i=4, t=PACK),
+                    in_=y_planes[:].rearrange("p t (c i) -> p c t i", i=4),
+                )
+                nc.vector.quantize_mx(
+                    out=y_words[:, g, :].bitcast(FP8X4), scales=y_scales[:, g, :], in_=y_grouped[:]
+                )
+            return y_words, y_scales
+
+        def project(group, y_words, y_scales):
+            for i in range(GROUP):
+                tok = slice(P * i, P * i + P)
+                z = z_pool.tile([P, H], F32, name="z")
+                z_sum = small.tile([P, HALVES], F32, name="z_sum")
+                for hh in range(HALVES):
+                    cols = slice(N_COLS * hh, N_COLS * (hh + 1))
+                    acc = psum_acc.tile([P, N_COLS], F32, name="acc")
+                    for g in range(PASSES):
+                        nc.tensor.matmul_mx(
+                            out=acc[:],
+                            lhsT=y_words[:, g, tok].bitcast(FP8X4),
+                            lhsT_scale=y_scales[:, g, tok],
+                            rhs=w_words[:, g, cols].bitcast(FP8X4),
+                            rhs_scale=w_scales[:, g, cols],
+                            start=(g == 0),
+                            stop=(g == PASSES - 1),
+                        )
+                    nc.vector.scalar_tensor_tensor(
+                        out=z[:, cols],
+                        in0=acc[:],
+                        scalar=1.0,
+                        in1=bias_b[:, cols],
+                        op0=ALU.mult,
+                        op1=ALU.add,
+                        accum_out=z_sum[:, hh : hh + 1],
+                    )
+                neg_mean = small.tile([P, 1], F32, name="neg_mean")
+                nc.vector.tensor_scalar(
+                    out=neg_mean[:],
+                    in0=z_sum[:, 0:1],
+                    scalar1=z_sum[:, 1:2],
+                    scalar2=-1.0 / H,
+                    op0=ALU.add,
+                    op1=ALU.mult,
+                )
+                squares = z_pool.tile([P, H], BF16, name="squares")
+                sum_sq = small.tile([P, 1], F32, name="sum_sq")
+                nc.scalar.activation(
+                    out=squares[:], in_=z[:], func=ACT.Square, bias=neg_mean[:], scale=1.0, accum_out=sum_sq[:]
+                )
+                std2 = small.tile([P, 1], F32, name="std2")
+                nc.scalar.activation(out=std2[:], in_=sum_sq[:], func=ACT.Sqrt, bias=eps_col[:], scale=1.0 / H)
+                rstd2 = small.tile([P, 1], F32, name="rstd2")
+                nc.vector.reciprocal(out=rstd2[:], in_=std2[:])
+                res = z_pool.tile([P, H], F32, name="res")
+                nc.vector.scalar_tensor_tensor(
+                    out=res[:], in0=z[:], scalar=neg_mean[:], in1=gain_b[:], op0=ALU.add, op1=ALU.mult
+                )
+                nc.vector.scalar_tensor_tensor(
+                    out=res[:], in0=res[:], scalar=rstd2[:], in1=shift_b[:], op0=ALU.mult, op1=ALU.add
+                )
+                nc.scalar.activation(out=res[:], in_=res[:], func=ACT.Relu)
+                first = GROUP_TOKENS * group + P * i
+                nc.sync.dma_start(out=out_rows[first : first + P, :], in_=res[:])
+
+        for i in range(GROUP):
+            normalise(i)
+            quantise_w(i)
+        for group in range(GROUPS):
+            if group + 1 < GROUPS:
+                for i in range(GROUP * (group + 1), GROUP * (group + 2)):
+                    load_x(i)
+            y_words, y_scales = quantise_y(group)
+            if group + 1 < GROUPS:
+                for i in range(GROUP * (group + 1), GROUP * (group + 2)):
+                    normalise(i)
+            project(group, y_words, y_scales)

@@ -21,12 +21,13 @@ PACK = 4
 K_PASS = P * PACK
 PASSES = C // K_PASS
 BLOCKS = C // P
+TILES = TOKENS // P
 GROUP = 4
 GROUP_TOKENS = GROUP * P
-GROUPS = TOKENS // GROUP_TOKENS
 N_COLS = 512
 HALVES = H // N_COLS
 BN_CHUNK = 512
+BIG = 3.0e38
 
 FLOPS = 2 * TOKENS * C * H
 
@@ -39,14 +40,15 @@ def tile_graphresblock_pa_kernel(tc, x, pre_w, pre_b, lin1_W, lin1_b, n1_w, n1_b
     with ExitStack() as stack:
         const = stack.enter_context(tc.tile_pool(name="const", bufs=1))
         small = stack.enter_context(tc.tile_pool(name="small", bufs=6))
-        x_pool = stack.enter_context(tc.tile_pool(name="x_pool", bufs=6))
+        x_pool = stack.enter_context(tc.tile_pool(name="x_pool", bufs=8))
         w_pool = stack.enter_context(tc.tile_pool(name="w_pool", bufs=4))
         xn_pool = stack.enter_context(tc.tile_pool(name="xn_pool", bufs=8))
         stage = stack.enter_context(tc.tile_pool(name="stage", bufs=3))
         y_pool = stack.enter_context(tc.tile_pool(name="y_pool", bufs=2))
         z_pool = stack.enter_context(tc.tile_pool(name="z_pool", bufs=3))
-        psum_t = stack.enter_context(tc.psum_pool(name="psum_t", bufs=4))
-        psum_acc = stack.enter_context(tc.psum_pool(name="psum_acc", bufs=4))
+        psum_const = stack.enter_context(tc.psum_pool(name="psum_const", bufs=1))
+        psum_t = stack.enter_context(tc.psum_pool(name="psum_t", bufs=3))
+        psum_acc = stack.enter_context(tc.psum_pool(name="psum_acc", bufs=3))
 
         ident = const.tile([P, P], F32)
         make_identity(nc, ident[:])
@@ -60,28 +62,32 @@ def tile_graphresblock_pa_kernel(tc, x, pre_w, pre_b, lin1_W, lin1_b, n1_w, n1_b
         nc.sync.dma_start(out=wb_rows[0:8, :], in_=pre_w.rearrange("(a c) -> a c", c=2 * P))
         nc.sync.dma_start(out=wb_rows[8:16, :], in_=pre_b.rearrange("(a c) -> a c", c=2 * P))
 
+        ones = const.tile([P, P], BF16)
+        nc.vector.memset(ones[:], 1.0)
+        n1_rows = const.tile([P, 2, H], BF16)
+        nc.vector.memset(n1_rows[:].rearrange("p v h -> p (v h)").bitcast(I32), 0)
+        nc.sync.dma_start(out=n1_rows[0:1, 0, :], in_=n1_w.rearrange("(o h) -> o h", o=1))
+        nc.sync.dma_start(out=n1_rows[0:1, 1, :], in_=n1_b.rearrange("(o h) -> o h", o=1))
         bias_b = const.tile([P, H], BF16)
-        gain_b = const.tile([P, H], BF16)
-        shift_b = const.tile([P, H], BF16)
-        nc.gpsimd.dma_start(out=bias_b[:], in_=lin1_b.partition_broadcast(P))
-        nc.gpsimd.dma_start(out=gain_b[:], in_=n1_w.partition_broadcast(P))
-        nc.gpsimd.dma_start(out=shift_b[:], in_=n1_b.partition_broadcast(P))
 
         x_nat = {}
         w_nat = {}
 
-        def load_x(i):
-            x_nat[i] = x_pool.tile([P, C], BF16, name="x_nat")
-            nc.sync.dma_start(out=x_nat[i][:], in_=x_rows[P * i : P * i + P, :])
+        def load_x(n):
+            x_nat[n] = x_pool.tile([P, C], BF16, name="x_nat")
+            nc.sync.dma_start(out=x_nat[n][:], in_=x_rows[P * n : P * n + P, :])
 
         def load_w(r):
             w_nat[r] = w_pool.tile([P, C], BF16, name="w_nat")
             nc.sync.dma_start(out=w_nat[r][:], in_=lin1_W[P * r : P * r + P, :])
 
-        for i in range(GROUP):
-            load_x(i)
-            load_w(2 * i)
-            load_w(2 * i + 1)
+        for n in range(GROUP):
+            load_x(n)
+            load_w(2 * n)
+            load_w(2 * n + 1)
+        nc.sync.dma_start(out=bias_b[:], in_=lin1_b.partition_broadcast(P))
+        for n in range(GROUP, TILES):
+            load_x(n)
 
         wb_t = psum_t.tile([P, N_COLS], F32, tag="t")
         nc.tensor.transpose(wb_t[:, 0:P], wb_rows[:].bitcast(F32), ident[:])
@@ -90,12 +96,19 @@ def tile_graphresblock_pa_kernel(tc, x, pre_w, pre_b, lin1_W, lin1_b, n1_w, n1_b
         wb_cols = const.tile([P, 2 * BLOCKS], F32)
         nc.vector.tensor_copy(out=wb_cols[:], in_=wb_pairs[:])
 
+        gain_b = psum_const.tile([P, H], BF16)
+        shift_b = psum_const.tile([P, H], BF16)
+        for hh in range(HALVES):
+            cols = slice(N_COLS * hh, N_COLS * (hh + 1))
+            nc.tensor.matmul(out=gain_b[:, cols], lhsT=ones[:], rhs=n1_rows[:, 0, cols], start=True, stop=True)
+            nc.tensor.matmul(out=shift_b[:, cols], lhsT=ones[:], rhs=n1_rows[:, 1, cols], start=True, stop=True)
+
         xn = {}
 
-        def normalise(i):
+        def normalise(n):
             stats = small.tile([P, C // BN_CHUNK, 6], F32, name="stats")
             for s in range(C // BN_CHUNK):
-                nc.vector.bn_stats(out=stats[:, s, :], in_=x_nat[i][:, BN_CHUNK * s : BN_CHUNK * (s + 1)])
+                nc.vector.bn_stats(out=stats[:, s, :], in_=x_nat[n][:, BN_CHUNK * s : BN_CHUNK * (s + 1)])
             mean_var = small.tile([P, 2], F32, name="mean_var")
             nc.vector.bn_aggr(out=mean_var[:], in_=stats[:].rearrange("p s d -> p (s d)"))
             std = small.tile([P, 1], F32, name="std")
@@ -106,13 +119,14 @@ def tile_graphresblock_pa_kernel(tc, x, pre_w, pre_b, lin1_W, lin1_b, n1_w, n1_b
             nc.vector.scalar_tensor_tensor(
                 out=shift[:], in0=mean_var[:, 0:1], scalar=-1.0, in1=rstd[:], op0=ALU.mult, op1=ALU.mult
             )
-            xn[i] = xn_pool.tile([P, BLOCKS, P], F32, name="xn")
-            nc.scalar.activation(
-                out=xn[i][:].rearrange("p (a e) q -> p a e q", e=2),
-                in_=x_nat[i][:].rearrange("p (a q e) -> p a e q", q=P, e=2),
-                func=ACT.Identity,
-                scale=rstd[:],
-                bias=shift[:],
+            xn[n] = xn_pool.tile([P, BLOCKS, P], F32, name="xn")
+            nc.gpsimd.tensor_scalar(
+                out=xn[n][:].rearrange("p (a e) q -> p a e q", e=2),
+                in0=x_nat[n][:].rearrange("p (a q e) -> p a e q", q=P, e=2),
+                scalar1=rstd[:],
+                scalar2=shift[:],
+                op0=ALU.mult,
+                op1=ALU.add,
             )
 
         w_words = const.tile([P, PASSES, H], U32, align_bytes=64)
@@ -136,98 +150,97 @@ def tile_graphresblock_pa_kernel(tc, x, pre_w, pre_b, lin1_W, lin1_b, n1_w, n1_b
                     out=w_words[:, g, cols].bitcast(FP8X4), scales=w_scales[:, g, cols], in_=w_grouped[:]
                 )
 
-        def quantise_y(group):
-            y_words = y_pool.tile([P, PASSES, GROUP_TOKENS], U32, align_bytes=64, name="y_words")
-            y_scales = y_pool.tile([P, PASSES, GROUP_TOKENS], U8, align_bytes=64, name="y_scales")
-            for g in range(PASSES):
-                y_planes = stage.tile([P, PACK, GROUP_TOKENS], BF16, name="y_planes")
-                for t in range(PACK):
-                    j = PACK * g + t
-                    xt = psum_t.tile([P, GROUP_TOKENS], F32, tag="t")
-                    for i in range(GROUP):
-                        nc.tensor.transpose(xt[:, P * i : P * i + P], xn[GROUP * group + i][:, j, :], ident[:])
-                    nc.scalar.activation(
-                        out=y_planes[:, t, :],
-                        in_=xt[:],
-                        func=ACT.Relu,
-                        scale=wb_cols[:, j : j + 1],
-                        bias=wb_cols[:, BLOCKS + j : BLOCKS + j + 1],
-                    )
-                y_grouped = stage.tile([P, GROUP_TOKENS * PACK], BF16, align_bytes=64, name="y_grouped")
-                nc.vector.tensor_copy(
-                    out=y_grouped[:].rearrange("p (c i t) -> p c t i", i=4, t=PACK),
-                    in_=y_planes[:].rearrange("p t (c i) -> p c t i", i=4),
-                )
-                nc.vector.quantize_mx(
-                    out=y_words[:, g, :].bitcast(FP8X4), scales=y_scales[:, g, :], in_=y_grouped[:]
-                )
-            return y_words, y_scales
+        y_words = {}
+        y_scales = {}
 
-        def project(group, y_words, y_scales):
-            for i in range(GROUP):
-                tok = slice(P * i, P * i + P)
-                z = z_pool.tile([P, H], F32, name="z")
-                z_sum = small.tile([P, HALVES], F32, name="z_sum")
-                for hh in range(HALVES):
-                    cols = slice(N_COLS * hh, N_COLS * (hh + 1))
-                    acc = psum_acc.tile([P, N_COLS], F32, name="acc")
-                    for g in range(PASSES):
-                        nc.tensor.matmul_mx(
-                            out=acc[:],
-                            lhsT=y_words[:, g, tok].bitcast(FP8X4),
-                            lhsT_scale=y_scales[:, g, tok],
-                            rhs=w_words[:, g, cols].bitcast(FP8X4),
-                            rhs_scale=w_scales[:, g, cols],
-                            start=(g == 0),
-                            stop=(g == PASSES - 1),
-                        )
-                    nc.vector.scalar_tensor_tensor(
-                        out=z[:, cols],
-                        in0=acc[:],
-                        scalar=1.0,
-                        in1=bias_b[:, cols],
-                        op0=ALU.mult,
-                        op1=ALU.add,
-                        accum_out=z_sum[:, hh : hh + 1],
-                    )
-                neg_mean = small.tile([P, 1], F32, name="neg_mean")
-                nc.vector.tensor_scalar(
-                    out=neg_mean[:],
-                    in0=z_sum[:, 0:1],
-                    scalar1=z_sum[:, 1:2],
-                    scalar2=-1.0 / H,
-                    op0=ALU.add,
-                    op1=ALU.mult,
-                )
-                squares = z_pool.tile([P, H], BF16, name="squares")
-                sum_sq = small.tile([P, 1], F32, name="sum_sq")
+        def quantise_y(group, g):
+            if g == 0:
+                y_words[group] = y_pool.tile([P, PASSES, GROUP_TOKENS], U32, align_bytes=64, name="y_words")
+                y_scales[group] = y_pool.tile([P, PASSES, GROUP_TOKENS], U8, align_bytes=64, name="y_scales")
+            y_planes = stage.tile([P, PACK, GROUP_TOKENS], BF16, name="y_planes")
+            for t in range(PACK):
+                j = PACK * g + t
+                xt = psum_t.tile([P, GROUP_TOKENS], F32, tag="t")
+                for i in range(GROUP):
+                    nc.tensor.transpose(xt[:, P * i : P * i + P], xn[GROUP * group + i][:, j, :], ident[:])
                 nc.scalar.activation(
-                    out=squares[:], in_=z[:], func=ACT.Square, bias=neg_mean[:], scale=1.0, accum_out=sum_sq[:]
+                    out=y_planes[:, t, :],
+                    in_=xt[:],
+                    func=ACT.Relu,
+                    scale=wb_cols[:, j : j + 1],
+                    bias=wb_cols[:, BLOCKS + j : BLOCKS + j + 1],
                 )
-                std2 = small.tile([P, 1], F32, name="std2")
-                nc.scalar.activation(out=std2[:], in_=sum_sq[:], func=ACT.Sqrt, bias=eps_col[:], scale=1.0 / H)
-                rstd2 = small.tile([P, 1], F32, name="rstd2")
-                nc.vector.reciprocal(out=rstd2[:], in_=std2[:])
-                res = z_pool.tile([P, H], F32, name="res")
-                nc.vector.scalar_tensor_tensor(
-                    out=res[:], in0=z[:], scalar=neg_mean[:], in1=gain_b[:], op0=ALU.add, op1=ALU.mult
-                )
-                nc.vector.scalar_tensor_tensor(
-                    out=res[:], in0=res[:], scalar=rstd2[:], in1=shift_b[:], op0=ALU.mult, op1=ALU.add
-                )
-                nc.scalar.activation(out=res[:], in_=res[:], func=ACT.Relu)
-                first = GROUP_TOKENS * group + P * i
-                nc.sync.dma_start(out=out_rows[first : first + P, :], in_=res[:])
+            y_grouped = stage.tile([P, GROUP_TOKENS * PACK], BF16, align_bytes=64, name="y_grouped")
+            nc.scalar.copy(
+                out=y_grouped[:].rearrange("p (c i t) -> p c t i", i=4, t=PACK),
+                in_=y_planes[:].rearrange("p t (c i) -> p c t i", i=4),
+            )
+            nc.vector.quantize_mx(
+                out=y_words[group][:, g, :].bitcast(FP8X4), scales=y_scales[group][:, g, :], in_=y_grouped[:]
+            )
 
-        for i in range(GROUP):
-            normalise(i)
-            quantise_w(i)
-        for group in range(GROUPS):
-            if group + 1 < GROUPS:
-                for i in range(GROUP * (group + 1), GROUP * (group + 2)):
-                    load_x(i)
-            y_words, y_scales = quantise_y(group)
-            if group + 1 < GROUPS:
-                for i in range(GROUP * (group + 1), GROUP * (group + 2)):
-                    normalise(i)
-            project(group, y_words, y_scales)
+        def project(n):
+            group = n // GROUP
+            tok = slice(P * (n % GROUP), P * (n % GROUP) + P)
+            z = z_pool.tile([P, H], F32, name="z")
+            z_sum = small.tile([P, HALVES], F32, name="z_sum")
+            for hh in range(HALVES):
+                cols = slice(N_COLS * hh, N_COLS * (hh + 1))
+                acc = psum_acc.tile([P, N_COLS], F32, name="acc")
+                for g in range(PASSES):
+                    nc.tensor.matmul_mx(
+                        out=acc[:],
+                        lhsT=y_words[group][:, g, tok].bitcast(FP8X4),
+                        lhsT_scale=y_scales[group][:, g, tok],
+                        rhs=w_words[:, g, cols].bitcast(FP8X4),
+                        rhs_scale=w_scales[:, g, cols],
+                        start=(g == 0),
+                        stop=(g == PASSES - 1),
+                    )
+                nc.vector.scalar_tensor_tensor(
+                    out=z[:, cols],
+                    in0=acc[:],
+                    scalar=1.0,
+                    in1=bias_b[:, cols],
+                    op0=ALU.mult,
+                    op1=ALU.add,
+                    accum_out=z_sum[:, hh : hh + 1],
+                )
+            neg_mean = small.tile([P, 1], F32, name="neg_mean")
+            nc.vector.tensor_scalar(
+                out=neg_mean[:],
+                in0=z_sum[:, 0:1],
+                scalar1=z_sum[:, 1:2],
+                scalar2=-1.0 / H,
+                op0=ALU.add,
+                op1=ALU.mult,
+            )
+            squares = z_pool.tile([P, H], BF16, name="squares")
+            sum_sq = small.tile([P, 1], F32, name="sum_sq")
+            nc.scalar.activation(
+                out=squares[:], in_=z[:], func=ACT.Square, bias=neg_mean[:], scale=1.0, accum_out=sum_sq[:]
+            )
+            std2 = small.tile([P, 1], F32, name="std2")
+            nc.scalar.activation(out=std2[:], in_=sum_sq[:], func=ACT.Sqrt, bias=eps_col[:], scale=1.0 / H)
+            rstd2 = small.tile([P, 1], F32, name="rstd2")
+            nc.vector.reciprocal(out=rstd2[:], in_=std2[:])
+            res = z_pool.tile([P, H], F32, name="res")
+            nc.vector.scalar_tensor_tensor(
+                out=res[:], in0=z[:], scalar=neg_mean[:], in1=gain_b[:], op0=ALU.add, op1=ALU.mult
+            )
+            nc.vector.scalar_tensor_tensor(
+                out=res[:], in0=res[:], scalar=rstd2[:], in1=shift_b[:], op0=ALU.mult, op1=ALU.add
+            )
+            nc.gpsimd.tensor_scalar(out=res[:], in0=res[:], scalar1=BIG, scalar2=0.0, op0=ALU.min, op1=ALU.max)
+            nc.sync.dma_start(out=out_rows[P * n : P * n + P, :], in_=res[:])
+
+        for n in range(GROUP):
+            normalise(n)
+            quantise_w(n)
+        for step in range(TILES + GROUP):
+            if step + GROUP < TILES:
+                normalise(step + GROUP)
+            if step < TILES:
+                quantise_y(step // PASSES, step % PASSES)
+            if step >= GROUP:
+                project(step - GROUP)

@@ -22,12 +22,12 @@ K_PASS = P * PACK
 PASSES = C // K_PASS
 BLOCKS = C // P
 TILES = TOKENS // P
+W_TILES = H // P
 GROUP = 4
 GROUP_TOKENS = GROUP * P
 N_COLS = 512
 HALVES = H // N_COLS
 BN_CHUNK = 512
-BIG = 3.0e38
 
 FLOPS = 2 * TOKENS * C * H
 
@@ -39,16 +39,14 @@ def tile_graphresblock_pa_kernel(tc, x, pre_w, pre_b, lin1_W, lin1_b, n1_w, n1_b
 
     with ExitStack() as stack:
         const = stack.enter_context(tc.tile_pool(name="const", bufs=1))
-        small = stack.enter_context(tc.tile_pool(name="small", bufs=6))
-        x_pool = stack.enter_context(tc.tile_pool(name="x_pool", bufs=8))
-        w_pool = stack.enter_context(tc.tile_pool(name="w_pool", bufs=4))
+        small = stack.enter_context(tc.tile_pool(name="small", bufs=8))
+        rows_pool = stack.enter_context(tc.tile_pool(name="rows_pool", bufs=12))
         xn_pool = stack.enter_context(tc.tile_pool(name="xn_pool", bufs=8))
         stage = stack.enter_context(tc.tile_pool(name="stage", bufs=3))
         y_pool = stack.enter_context(tc.tile_pool(name="y_pool", bufs=2))
         z_pool = stack.enter_context(tc.tile_pool(name="z_pool", bufs=3))
-        psum_const = stack.enter_context(tc.psum_pool(name="psum_const", bufs=1))
-        psum_t = stack.enter_context(tc.psum_pool(name="psum_t", bufs=3))
-        psum_acc = stack.enter_context(tc.psum_pool(name="psum_acc", bufs=3))
+        psum_t = stack.enter_context(tc.psum_pool(name="psum_t", bufs=4))
+        psum_acc = stack.enter_context(tc.psum_pool(name="psum_acc", bufs=4))
 
         ident = const.tile([P, P], F32)
         make_identity(nc, ident[:])
@@ -56,36 +54,32 @@ def tile_graphresblock_pa_kernel(tc, x, pre_w, pre_b, lin1_W, lin1_b, n1_w, n1_b
         nc.vector.memset(eps_col[:], EPS)
         table_warm = const.tile([P, 1], F32)
         nc.scalar.activation(out=table_warm[:], in_=eps_col[:], func=ACT.Sqrt)
-
-        wb_rows = const.tile([P, 2 * P], BF16)
-        nc.vector.memset(wb_rows[:].bitcast(I32), 0)
-        nc.sync.dma_start(out=wb_rows[0:8, :], in_=pre_w.rearrange("(a c) -> a c", c=2 * P))
-        nc.sync.dma_start(out=wb_rows[8:16, :], in_=pre_b.rearrange("(a c) -> a c", c=2 * P))
-
         ones = const.tile([P, P], BF16)
         nc.vector.memset(ones[:], 1.0)
-        n1_rows = const.tile([P, 2, H], BF16)
-        nc.vector.memset(n1_rows[:].rearrange("p v h -> p (v h)").bitcast(I32), 0)
-        nc.sync.dma_start(out=n1_rows[0:1, 0, :], in_=n1_w.rearrange("(o h) -> o h", o=1))
-        nc.sync.dma_start(out=n1_rows[0:1, 1, :], in_=n1_b.rearrange("(o h) -> o h", o=1))
-        bias_b = const.tile([P, H], BF16)
+        wb_rows = const.tile([P, 2 * P], BF16)
+        nc.vector.memset(wb_rows[:].bitcast(I32), 0)
+        vec_rows = const.tile([P, 3, H], BF16)
+        nc.vector.memset(vec_rows[:].rearrange("p v h -> p (v h)").bitcast(I32), 0)
 
         x_nat = {}
         w_nat = {}
 
         def load_x(n):
-            x_nat[n] = x_pool.tile([P, C], BF16, name="x_nat")
+            x_nat[n] = rows_pool.tile([P, C], BF16, name="x_nat", tag="rows")
             nc.sync.dma_start(out=x_nat[n][:], in_=x_rows[P * n : P * n + P, :])
 
         def load_w(r):
-            w_nat[r] = w_pool.tile([P, C], BF16, name="w_nat")
+            w_nat[r] = rows_pool.tile([P, C], BF16, name="w_nat", tag="rows")
             nc.sync.dma_start(out=w_nat[r][:], in_=lin1_W[P * r : P * r + P, :])
 
         for n in range(GROUP):
             load_x(n)
-            load_w(2 * n)
-            load_w(2 * n + 1)
-        nc.sync.dma_start(out=bias_b[:], in_=lin1_b.partition_broadcast(P))
+        nc.sync.dma_start(out=wb_rows[0:8, :], in_=pre_w.rearrange("(a c) -> a c", c=2 * P))
+        nc.sync.dma_start(out=wb_rows[8:16, :], in_=pre_b.rearrange("(a c) -> a c", c=2 * P))
+        for r in range(W_TILES):
+            load_w(r)
+        for v, vec in enumerate((lin1_b, n1_w, n1_b)):
+            nc.sync.dma_start(out=vec_rows[0:1, v, :], in_=vec.rearrange("(o h) -> o h", o=1))
         for n in range(GROUP, TILES):
             load_x(n)
 
@@ -95,13 +89,6 @@ def tile_graphresblock_pa_kernel(tc, x, pre_w, pre_b, lin1_W, lin1_b, n1_w, n1_b
         nc.vector.tensor_copy(out=wb_pairs[:].bitcast(F32), in_=wb_t[:, 0:BLOCKS])
         wb_cols = const.tile([P, 2 * BLOCKS], F32)
         nc.vector.tensor_copy(out=wb_cols[:], in_=wb_pairs[:])
-
-        gain_b = psum_const.tile([P, H], BF16)
-        shift_b = psum_const.tile([P, H], BF16)
-        for hh in range(HALVES):
-            cols = slice(N_COLS * hh, N_COLS * (hh + 1))
-            nc.tensor.matmul(out=gain_b[:, cols], lhsT=ones[:], rhs=n1_rows[:, 0, cols], start=True, stop=True)
-            nc.tensor.matmul(out=shift_b[:, cols], lhsT=ones[:], rhs=n1_rows[:, 1, cols], start=True, stop=True)
 
         xn = {}
 
@@ -120,13 +107,12 @@ def tile_graphresblock_pa_kernel(tc, x, pre_w, pre_b, lin1_W, lin1_b, n1_w, n1_b
                 out=shift[:], in0=mean_var[:, 0:1], scalar=-1.0, in1=rstd[:], op0=ALU.mult, op1=ALU.mult
             )
             xn[n] = xn_pool.tile([P, BLOCKS, P], F32, name="xn")
-            nc.gpsimd.tensor_scalar(
+            nc.scalar.activation(
                 out=xn[n][:].rearrange("p (a e) q -> p a e q", e=2),
-                in0=x_nat[n][:].rearrange("p (a q e) -> p a e q", q=P, e=2),
-                scalar1=rstd[:],
-                scalar2=shift[:],
-                op0=ALU.mult,
-                op1=ALU.add,
+                in_=x_nat[n][:].rearrange("p (a q e) -> p a e q", q=P, e=2),
+                func=ACT.Identity,
+                scale=rstd[:],
+                bias=shift[:],
             )
 
         w_words = const.tile([P, PASSES, H], U32, align_bytes=64)
@@ -150,6 +136,15 @@ def tile_graphresblock_pa_kernel(tc, x, pre_w, pre_b, lin1_W, lin1_b, n1_w, n1_b
                     out=w_words[:, g, cols].bitcast(FP8X4), scales=w_scales[:, g, cols], in_=w_grouped[:]
                 )
 
+        def spread(v):
+            spread_ps = psum_t.tile([P, H], BF16, tag="t")
+            for hh in range(HALVES):
+                cols = slice(N_COLS * hh, N_COLS * (hh + 1))
+                nc.tensor.matmul(out=spread_ps[:, cols], lhsT=ones[:], rhs=vec_rows[:, v, cols], start=True, stop=True)
+            spread_sb = const.tile([P, H], BF16, name="spread_sb%d" % v)
+            nc.scalar.copy(out=spread_sb[:], in_=spread_ps[:])
+            return spread_sb
+
         y_words = {}
         y_scales = {}
 
@@ -171,7 +166,7 @@ def tile_graphresblock_pa_kernel(tc, x, pre_w, pre_b, lin1_W, lin1_b, n1_w, n1_b
                     bias=wb_cols[:, BLOCKS + j : BLOCKS + j + 1],
                 )
             y_grouped = stage.tile([P, GROUP_TOKENS * PACK], BF16, align_bytes=64, name="y_grouped")
-            nc.scalar.copy(
+            nc.vector.tensor_copy(
                 out=y_grouped[:].rearrange("p (c i t) -> p c t i", i=4, t=PACK),
                 in_=y_planes[:].rearrange("p t (c i) -> p c t i", i=4),
             )
@@ -231,12 +226,16 @@ def tile_graphresblock_pa_kernel(tc, x, pre_w, pre_b, lin1_W, lin1_b, n1_w, n1_b
             nc.vector.scalar_tensor_tensor(
                 out=res[:], in0=res[:], scalar=rstd2[:], in1=shift_b[:], op0=ALU.mult, op1=ALU.add
             )
-            nc.gpsimd.tensor_scalar(out=res[:], in0=res[:], scalar1=BIG, scalar2=0.0, op0=ALU.min, op1=ALU.max)
+            nc.scalar.activation(out=res[:], in_=res[:], func=ACT.Relu)
             nc.sync.dma_start(out=out_rows[P * n : P * n + P, :], in_=res[:])
 
         for n in range(GROUP):
             normalise(n)
-            quantise_w(n)
+        for pair in range(W_TILES // 2):
+            quantise_w(pair)
+        bias_b = spread(0)
+        gain_b = spread(1)
+        shift_b = spread(2)
         for step in range(TILES + GROUP):
             if step + GROUP < TILES:
                 normalise(step + GROUP)

from contextlib import ExitStack

import concourse.mybir as mybir
from concourse.masks import make_identity

F32 = mybir.dt.float32
BF16 = mybir.dt.bfloat16
I32 = mybir.dt.int32
U32 = mybir.dt.uint32
U8 = mybir.dt.uint8
FP8X4 = mybir.dt.float8_e4m3fn_x4
ACT = mybir.ActivationFunctionType
ALU = mybir.AluOpType

P = 128
TOKENS = 1536
C = 2048
H = 1024
EPS = 1e-12
PACK = 4
K_PASS = P * PACK
PASSES = C // K_PASS
BLOCKS = C // P
TILES = TOKENS // P
W_TILES = H // P
GROUP = 4
GROUP_TOKENS = GROUP * P
N_COLS = 512
HALVES = H // N_COLS
BN_CHUNK = 512

FLOPS = 2 * TOKENS * C * H


def tile_graphresblock_pa_kernel(tc, x, pre_w, pre_b, lin1_W, lin1_b, n1_w, n1_b, out):
    nc = tc.nc
    x_rows = x.flatten_outer_dims()
    out_rows = out.flatten_outer_dims()

    with ExitStack() as stack:
        const = stack.enter_context(tc.tile_pool(name="const", bufs=1))
        small = stack.enter_context(tc.tile_pool(name="small", bufs=8))
        rows_pool = stack.enter_context(tc.tile_pool(name="rows_pool", bufs=12))
        xn_pool = stack.enter_context(tc.tile_pool(name="xn_pool", bufs=8))
        stage = stack.enter_context(tc.tile_pool(name="stage", bufs=3))
        y_pool = stack.enter_context(tc.tile_pool(name="y_pool", bufs=2))
        z_pool = stack.enter_context(tc.tile_pool(name="z_pool", bufs=3))
        psum_t = stack.enter_context(tc.psum_pool(name="psum_t", bufs=4))
        psum_acc = stack.enter_context(tc.psum_pool(name="psum_acc", bufs=4))

        ident = const.tile([P, P], F32)
        make_identity(nc, ident[:])
        eps_col = const.tile([P, 1], F32)
        nc.vector.memset(eps_col[:], EPS)
        table_warm = const.tile([P, 1], F32)
        nc.scalar.activation(out=table_warm[:], in_=eps_col[:], func=ACT.Sqrt)
        ones = const.tile([P, P], BF16)
        nc.vector.memset(ones[:], 1.0)
        wb_rows = const.tile([P, 2 * P], BF16)
        nc.vector.memset(wb_rows[:].bitcast(I32), 0)
        vec_rows = const.tile([P, 3, H], BF16)
        nc.vector.memset(vec_rows[:].rearrange("p v h -> p (v h)").bitcast(I32), 0)

        x_nat = {}
        w_nat = {}

        def load_x(n):
            x_nat[n] = rows_pool.tile([P, C], BF16, name="x_nat", tag="rows")
            nc.sync.dma_start(out=x_nat[n][:], in_=x_rows[P * n : P * n + P, :])

        def load_w(r):
            w_nat[r] = rows_pool.tile([P, C], BF16, name="w_nat", tag="rows")
            nc.sync.dma_start(out=w_nat[r][:], in_=lin1_W[P * r : P * r + P, :])

        for n in range(GROUP):
            load_x(n)
        nc.sync.dma_start(out=wb_rows[0:8, :], in_=pre_w.rearrange("(a c) -> a c", c=2 * P))
        nc.sync.dma_start(out=wb_rows[8:16, :], in_=pre_b.rearrange("(a c) -> a c", c=2 * P))
        for r in range(W_TILES):
            load_w(r)
        for v, vec in enumerate((lin1_b, n1_w, n1_b)):
            nc.sync.dma_start(out=vec_rows[0:1, v, :], in_=vec.rearrange("(o h) -> o h", o=1))
        for n in range(GROUP, TILES):
            load_x(n)

        wb_t = psum_t.tile([P, N_COLS], F32, tag="t")
        nc.tensor.transpose(wb_t[:, 0:P], wb_rows[:].bitcast(F32), ident[:])
        wb_pairs = const.tile([P, 2 * BLOCKS], BF16)
        nc.vector.tensor_copy(out=wb_pairs[:].bitcast(F32), in_=wb_t[:, 0:BLOCKS])
        wb_cols = const.tile([P, 2 * BLOCKS], F32)
        nc.vector.tensor_copy(out=wb_cols[:], in_=wb_pairs[:])

        xn = {}

        def normalise(n):
            stats = small.tile([P, C // BN_CHUNK, 6], F32, name="stats")
            for s in range(C // BN_CHUNK):
                nc.vector.bn_stats(out=stats[:, s, :], in_=x_nat[n][:, BN_CHUNK * s : BN_CHUNK * (s + 1)])
            mean_var = small.tile([P, 2], F32, name="mean_var")
            nc.vector.bn_aggr(out=mean_var[:], in_=stats[:].rearrange("p s d -> p (s d)"))
            std = small.tile([P, 1], F32, name="std")
            nc.scalar.activation(out=std[:], in_=mean_var[:, 1:2], func=ACT.Sqrt, bias=eps_col[:], scale=1.0)
            rstd = small.tile([P, 1], F32, name="rstd")
            nc.vector.reciprocal(out=rstd[:], in_=std[:])
            shift = small.tile([P, 1], F32, name="shift")
            nc.vector.scalar_tensor_tensor(
                out=shift[:], in0=mean_var[:, 0:1], scalar=-1.0, in1=rstd[:], op0=ALU.mult, op1=ALU.mult
            )
            xn[n] = xn_pool.tile([P, BLOCKS, P], F32, name="xn")
            nc.scalar.activation(
                out=xn[n][:].rearrange("p (a e) q -> p a e q", e=2),
                in_=x_nat[n][:].rearrange("p (a q e) -> p a e q", q=P, e=2),
                func=ACT.Identity,
                scale=rstd[:],
                bias=shift[:],
            )

        w_words = const.tile([P, PASSES, H], U32, align_bytes=64)
        w_scales = const.tile([P, PASSES, H], U8, align_bytes=64)

        def quantise_w(pair):
            for g in range(PASSES):
                wt = psum_t.tile([P, 2, 2 * P], F32, tag="t")
                for u in range(2):
                    for r in range(2):
                        words = w_nat[2 * pair + r][:].bitcast(F32)
                        first = P * (2 * g + u)
                        nc.tensor.transpose(wt[:, u, P * r : P * r + P], words[:, first : first + P], ident[:])
                w_grouped = stage.tile([P, 2 * P * PACK], BF16, align_bytes=64, name="w_grouped")
                nc.scalar.copy(
                    out=w_grouped[:].bitcast(F32).rearrange("p (h u) -> p h u", u=2),
                    in_=wt[:].rearrange("p u h -> p h u"),
                )
                cols = slice(2 * P * pair, 2 * P * (pair + 1))
                nc.vector.quantize_mx(
                    out=w_words[:, g, cols].bitcast(FP8X4), scales=w_scales[:, g, cols], in_=w_grouped[:]
                )

        def spread(v):
            spread_ps = psum_t.tile([P, H], BF16, tag="t")
            for hh in range(HALVES):
                cols = slice(N_COLS * hh, N_COLS * (hh + 1))
                nc.tensor.matmul(out=spread_ps[:, cols], lhsT=ones[:], rhs=vec_rows[:, v, cols], start=True, stop=True)
            spread_sb = const.tile([P, H], BF16, name="spread_sb%d" % v)
            nc.scalar.copy(out=spread_sb[:], in_=spread_ps[:])
            return spread_sb

        y_words = {}
        y_scales = {}

        def quantise_y(group, g):
            if g == 0:
                y_words[group] = y_pool.tile([P, PASSES, GROUP_TOKENS], U32, align_bytes=64, name="y_words")
                y_scales[group] = y_pool.tile([P, PASSES, GROUP_TOKENS], U8, align_bytes=64, name="y_scales")
            y_planes = stage.tile([P, PACK, GROUP_TOKENS], BF16, name="y_planes")
            for t in range(PACK):
                j = PACK * g + t
                xt = psum_t.tile([P, GROUP_TOKENS], F32, tag="t")
                for i in range(GROUP):
                    nc.tensor.transpose(xt[:, P * i : P * i + P], xn[GROUP * group + i][:, j, :], ident[:])
                nc.scalar.activation(
                    out=y_planes[:, t, :],
                    in_=xt[:],
                    func=ACT.Relu,
                    scale=wb_cols[:, j : j + 1],
                    bias=wb_cols[:, BLOCKS + j : BLOCKS + j + 1],
                )
            y_grouped = stage.tile([P, GROUP_TOKENS * PACK], BF16, align_bytes=64, name="y_grouped")
            nc.vector.tensor_copy(
                out=y_grouped[:].rearrange("p (c i t) -> p c t i", i=4, t=PACK),
                in_=y_planes[:].rearrange("p t (c i) -> p c t i", i=4),
            )
            nc.vector.quantize_mx(
                out=y_words[group][:, g, :].bitcast(FP8X4), scales=y_scales[group][:, g, :], in_=y_grouped[:]
            )

        def project(n):
            group = n // GROUP
            tok = slice(P * (n % GROUP), P * (n % GROUP) + P)
            z = z_pool.tile([P, H], F32, name="z")
            z_sum = small.tile([P, HALVES], F32, name="z_sum")
            for hh in range(HALVES):
                cols = slice(N_COLS * hh, N_COLS * (hh + 1))
                acc = psum_acc.tile([P, N_COLS], F32, name="acc")
                for g in range(PASSES):
                    nc.tensor.matmul_mx(
                        out=acc[:],
                        lhsT=y_words[group][:, g, tok].bitcast(FP8X4),
                        lhsT_scale=y_scales[group][:, g, tok],
                        rhs=w_words[:, g, cols].bitcast(FP8X4),
                        rhs_scale=w_scales[:, g, cols],
                        start=(g == 0),
                        stop=(g == PASSES - 1),
                    )
                nc.vector.scalar_tensor_tensor(
                    out=z[:, cols],
                    in0=acc[:],
                    scalar=1.0,
                    in1=bias_b[:, cols],
                    op0=ALU.mult,
                    op1=ALU.add,
                    accum_out=z_sum[:, hh : hh + 1],
                )
            neg_mean = small.tile([P, 1], F32, name="neg_mean")
            nc.vector.tensor_scalar(
                out=neg_mean[:],
                in0=z_sum[:, 0:1],
                scalar1=z_sum[:, 1:2],
                scalar2=-1.0 / H,
                op0=ALU.add,
                op1=ALU.mult,
            )
            squares = z_pool.tile([P, H], BF16, name="squares")
            sum_sq = small.tile([P, 1], F32, name="sum_sq")
            nc.scalar.activation(
                out=squares[:], in_=z[:], func=ACT.Square, bias=neg_mean[:], scale=1.0, accum_out=sum_sq[:]
            )
            std2 = small.tile([P, 1], F32, name="std2")
            nc.scalar.activation(out=std2[:], in_=sum_sq[:], func=ACT.Sqrt, bias=eps_col[:], scale=1.0 / H)
            rstd2 = small.tile([P, 1], F32, name="rstd2")
            nc.vector.reciprocal(out=rstd2[:], in_=std2[:])
            res = z_pool.tile([P, H], F32, name="res")
            nc.vector.scalar_tensor_tensor(
                out=res[:], in0=z[:], scalar=neg_mean[:], in1=gain_b[:], op0=ALU.add, op1=ALU.mult
            )
            nc.vector.scalar_tensor_tensor(
                out=res[:], in0=res[:], scalar=rstd2[:], in1=shift_b[:], op0=ALU.mult, op1=ALU.add
            )
            nc.scalar.activation(out=res[:], in_=res[:], func=ACT.Relu)
            nc.sync.dma_start(out=out_rows[P * n : P * n + P, :], in_=res[:])

        for n in range(GROUP):
            normalise(n)
        for pair in range(W_TILES // 2):
            quantise_w(pair)
        bias_b = spread(0)
        gain_b = spread(1)
        shift_b = spread(2)
        for step in range(TILES + GROUP):
            if step + GROUP < TILES:
                normalise(step + GROUP)
            if step < TILES:
                quantise_y(step // PASSES, step % PASSES)
            if step >= GROUP:
                project(step - GROUP)
